import numpy as np
import ml_dtypes


def mxq(x, axis, fmt="e4m3"):
    dtype, down = {"e4m3": (ml_dtypes.float8_e4m3fn, 7), "e5m2": (ml_dtypes.float8_e5m2, 14)}[fmt]
    v = np.moveaxis(np.asarray(x, np.float32).astype(ml_dtypes.bfloat16).astype(np.float64), axis, -1)
    blocks = v.reshape(v.shape[:-1] + (-1, 32))
    amax = np.abs(blocks).max(-1, keepdims=True)
    byte = np.maximum(np.where(amax > 0, np.frexp(amax)[1] - 1 + 127, 0) - down, 1)
    scale = np.exp2(byte - 127.0)
    codes = (blocks / scale).astype(np.float32).astype(dtype).astype(np.float64)
    return np.moveaxis((codes * scale).reshape(v.shape), -1, axis)


WIDE = False


def mx_kscale(k):
    if not WIDE:
        return np.ones(k)
    levels = np.array([10, -10, 5, -5, 0])
    if k % 512:
        return np.exp2(np.random.permutation(np.resize(levels, k // 32))).repeat(32)
    a = np.empty((k // 512, 16))
    for p in range(k // 512):
        a[p, :8] = np.random.permutation(np.resize(levels, 8))
        for g in range(8):
            far = levels[np.abs(levels - a[p, g]) >= 10]
            a[p, g + 8] = far[np.random.randint(len(far))]
    return np.exp2(a.ravel()).repeat(32)


BF16 = ml_dtypes.bfloat16


def bf(x):
    return np.asarray(x, np.float32).astype(BF16)


def f64(x):
    return np.asarray(x).astype(np.float64)


B, H0, C0, C1, C2, NA, NO = 2, 32, 512, 512, 1024, 3, 128
H1, H2 = H0 // 2, H0 // 4
O = NA * NO


def sigmoid(v):
    return 1.0 / (1.0 + np.exp(-v))


def _draw_level(c, h):
    s = mx_kscale(c)
    f = bf(np.random.standard_normal((B, c, h, h)) * s[None, :, None, None])
    w = bf(np.random.standard_normal((O, c)) / np.sqrt(c) / s[None, :])
    b = bf(np.random.standard_normal(O) * 0.5)
    return f, w, b


def setup_inputs():
    f0, w0, b0 = _draw_level(C0, H0)
    f1, w1, b1 = _draw_level(C1, H1)
    f2, w2, b2 = _draw_level(C2, H2)
    anchors = bf(1.0 + 4.0 * np.random.random((3, NA, 2)))
    return {"f0": f0, "f1": f1, "f2": f2, "w0": w0, "b0": b0, "w1": w1, "b1": b1, "w2": w2, "b2": b2, "anchors": anchors}


def _decode_level(f, w, b, anchors_i):
    nb, c, h, wd = f.shape
    y = (mxq(w, 1, "e4m3") @ mxq(f.reshape(nb, c, h * wd), 1, "e4m3")) + b[None, :, None]
    y = y.reshape(nb, NA, NO, h, wd).transpose(0, 1, 3, 4, 2)
    xy = 2.0 * sigmoid(y[..., 0:2]) - 0.5
    wh = np.square(2.0 * sigmoid(y[..., 2:4])) * anchors_i[None, :, None, None, :]
    rest = y[..., 4:]
    out = np.concatenate([xy, wh, rest], axis=-1)
    return out.reshape(nb, -1, NO)


def core(f0, f1, f2, w0, b0, w1, b1, w2, b2, anchors):
    a = f64(anchors)
    outs = [
        _decode_level(f64(f0), f64(w0), f64(b0), a[0]),
        _decode_level(f64(f1), f64(w1), f64(b1), a[1]),
        _decode_level(f64(f2), f64(w2), f64(b2), a[2]),
    ]
    return np.concatenate(outs, axis=1)


def e4m3fn_bytes(y):
    return np.clip(np.asarray(y, np.float64), -448.0, 448.0).astype(np.float32).astype(ml_dtypes.float8_e4m3fn).view(np.uint8)


def reference(f0, f1, f2, w0, b0, w1, b1, w2, b2, anchors):
    out = core(f0, f1, f2, w0, b0, w1, b1, w2, b2, anchors)
    s = np.max(np.abs(out)) / 448.0
    return out, e4m3fn_bytes(out / s)

@@ -1,0 +1,366 @@
+from contextlib import ExitStack
+
+import concourse.mybir as mybir
+from concourse.masks import make_identity
+
+F32 = mybir.dt.float32
+BF16 = mybir.dt.bfloat16
+U32 = mybir.dt.uint32
+U8 = mybir.dt.uint8
+FP8X4 = mybir.dt.float8_e4m3fn_x4
+FP8 = mybir.dt.float8_e4m3fn
+ALU = mybir.AluOpType
+ACT = mybir.ActivationFunctionType
+AX = mybir.AxisListType
+
+P = 128
+PACK = 4
+NA = 3
+O = NA * P
+ROWS_1 = 3072
+ROWS_2 = 3840
+FP8_MAX = 448.0
+
+FLOPS = 2 * O * (512 * 2048 + 512 * 512 + 1024 * 128)
+
+CODE_COLUMNS = [512, 512, 512, 512, 512, 256]
+RESULT_COLUMNS = [4 * O, 4 * O, 4 * O, 4 * O, 4 * O, O]
+
+
+def tile_head_kernel(tc, f0, f1, f2, w0, b0, w1, b1, w2, b2, anchors, out_0, out_1):
+    nc = tc.nc
+    with ExitStack() as ctx:
+        keep = ctx.enter_context(tc.tile_pool(name="keep", bufs=1))
+        ps_turn = ctx.enter_context(tc.psum_pool(name="ps_turn", bufs=5))
+        ps_acc = ctx.enter_context(tc.psum_pool(name="ps_acc", bufs=3))
+        ctx.enter_context(tc.manual_schedule())
+
+        b0_row = keep.tile([1, O], BF16, name="b0_row")
+        nc.sync.dma_start(out=b0_row[0:1, :], in_=b0.rearrange("(x o) -> x o", x=1))
+        anchors_bf = keep.tile([P, 18], BF16, name="anchors_bf")
+        nc.scalar.dma_start(out=anchors_bf[:], in_=anchors.rearrange("l a c -> (l a c)").partition_broadcast(P))
+        w0_raw = keep.tile([P, NA, 512], BF16, name="w0_raw")
+        f0_raw = []
+        for n in range(2):
+            image = f0[n].rearrange("(p j) u v -> p j (u v)", j=PACK)
+            for h in range(2):
+                half = keep.tile([P, PACK, 512], BF16, name="f0_raw%d%d" % (n, h))
+                nc.sync.dma_start(out=half[:], in_=image[:, :, 512 * h : 512 * (h + 1)])
+                f0_raw.append(half)
+                if n == 0 and h == 0:
+                    nc.sync.dma_start(out=w0_raw[:], in_=w0.rearrange("(a p) k -> p a k", p=P))
+        w1_raw = keep.tile([P, NA, 512], BF16, name="w1_raw")
+        nc.sync.dma_start(out=w1_raw[:], in_=w1.rearrange("(a p) k -> p a k", p=P))
+        w2_raw = keep.tile([P, NA, 1024], BF16, name="w2_raw")
+        nc.sync.dma_start(out=w2_raw[:], in_=w2.rearrange("(a p) k -> p a k", p=P))
+        f1_raw = keep.tile([P, 2, PACK, 256], BF16, name="f1_raw")
+        nc.sync.dma_start(
+            out=f1_raw[:].rearrange("p n j w -> p n (j w)"),
+            in_=f1.rearrange("n (p j) u v -> p n (j u v)", j=PACK),
+        )
+        f2_raw = keep.tile([P, 2, 2, PACK, 64], BF16, name="f2_raw")
+        for n in range(2):
+            nc.sync.dma_start(
+                out=f2_raw[:, n].rearrange("p s j w -> p s (j w)"),
+                in_=f2[n].rearrange("(s p j) u v -> p s (j u v)", s=2, j=PACK),
+            )
+        bias12 = keep.tile([P, 2, O], BF16, name="bias12")
+        nc.sync.dma_start(out=bias12[:, 0, :], in_=b1.partition_broadcast(P))
+        nc.sync.dma_start(out=bias12[:, 1, :], in_=b2.partition_broadcast(P))
+
+        zero = keep.tile([P, 1], F32, name="zero")
+        nc.vector.memset(zero[:], 0.0)
+        warm = keep.tile([P, 1], F32, name="warm")
+        nc.scalar.activation(out=warm[:], in_=zero[:], func=ACT.Sigmoid)
+        b0_rows = keep.tile([P, O], BF16, name="b0_rows")
+        nc.vector.memset(b0_rows[:], 0.0)
+        ones = keep.tile([P, P], BF16, name="ones")
+        nc.vector.memset(ones[:], 1.0)
+        ident = keep.tile([P, P], F32, name="ident")
+        make_identity(nc, ident[:])
+        nc.vector.tensor_copy(out=b0_rows[0:1, :], in_=b0_row[0:1, :])
+
+        bias0 = keep.tile([P, O], F32, name="bias0")
+        anchors_x4 = keep.tile([P, 18], F32, name="anchors_x4")
+        anchors_0 = keep.tile([P, NA, 4, 2], F32, name="anchors_0")
+        anchors_1 = keep.tile([P, 2, NA, 2, 2], F32, name="anchors_1")
+
+        def spread_bias0():
+            bank = ps_turn.tile([P, 512], F32, name="bank", tag="turn")
+            nc.tensor.matmul(bank[:, 0:O], lhsT=ones[:], rhs=b0_rows[:], start=True, stop=True)
+            nc.scalar.copy(out=bias0[:], in_=bank[:, 0:O])
+
+        def spread_anchors():
+            nc.scalar.activation(out=anchors_x4[:], in_=anchors_bf[:], func=ACT.Copy, scale=4.0)
+            for r in range(4):
+                nc.gpsimd.tensor_copy(
+                    out=anchors_0[:, :, r, :], in_=anchors_x4[:, 0:6].rearrange("p (a c) -> p a c", c=2)
+                )
+            for n in range(2):
+                for r in range(2):
+                    nc.gpsimd.tensor_copy(
+                        out=anchors_1[:, n, :, r, :], in_=anchors_x4[:, 6:12].rearrange("p (a c) -> p a c", c=2)
+                    )
+
+        def turn_weights(units, grouped, first):
+            words_out = grouped[:].bitcast(F32).rearrange("p (q r u) -> p q r u", r=P, u=2)
+            turned = ps_turn.tile([P, 2, 2, P], F32, name="turned", tag="turn")
+            for i, (raw, a, s) in enumerate(units):
+                words = raw[:, a, :].bitcast(F32)
+                for u in range(2):
+                    nc.tensor.transpose(turned[:, i, u, :], words[:, 256 * s + u : 256 * (s + 1) : 2], ident[:])
+            nc.scalar.copy(
+                out=words_out[:, first : first + len(units), :, :],
+                in_=turned[:, 0 : len(units)].rearrange("p i u r -> p i r u"),
+            )
+
+        def quantize(grouped, codes, scales, c0, c1):
+            nc.vector.quantize_mx(
+                out=codes[:, c0:c1].bitcast(FP8X4),
+                scales=scales[:, c0:c1],
+                in_=grouped[:, PACK * c0 : PACK * c1],
+            )
+
+        w0_grouped = keep.tile([P, PACK * O], BF16, name="w0_grouped", align_bytes=64)
+        w0_codes = keep.tile([P, O], U32, name="w0_codes", align_bytes=64)
+        w0_scales = keep.tile([P, O], U8, name="w0_scales", align_bytes=64)
+        w12_grouped = keep.tile([P, PACK * 3 * O], BF16, name="w12_grouped", align_bytes=64)
+        w12_codes = keep.tile([P, 3 * O], U32, name="w12_codes", align_bytes=64)
+        w12_scales = keep.tile([P, 3 * O], U8, name="w12_scales", align_bytes=64)
+        w0_units = [(w0_raw, a, 0) for a in range(NA)]
+        w12_units = [(w1_raw, a, 0) for a in range(NA)] + [(w2_raw, a, s) for s in range(2) for a in range(NA)]
+
+        def turn_w12(pair):
+            turn_weights(w12_units[2 * pair : 2 * pair + 2], w12_grouped, 2 * pair)
+
+        maxima = keep.tile([P, 8], F32, name="maxima")
+        f_grouped = [
+            keep.tile([P, PACK * c], BF16, name="f_grouped%d" % g, align_bytes=64) for g, c in enumerate(CODE_COLUMNS)
+        ]
+        f_codes = [keep.tile([P, c], U32, name="f_codes%d" % g, align_bytes=64) for g, c in enumerate(CODE_COLUMNS)]
+        f_scales = [keep.tile([P, c], U8, name="f_scales%d" % g, align_bytes=64) for g, c in enumerate(CODE_COLUMNS)]
+        result = [keep.tile([P, c], F32, name="result%d" % g) for g, c in enumerate(RESULT_COLUMNS)]
+        result_fp8 = [keep.tile([P, c], FP8, name="result_fp8_%d" % g) for g, c in enumerate(RESULT_COLUMNS)]
+
+        def interleave(g, copy, first, last):
+            if g < 4:
+                part = slice(64 * first, 64 * (last + 1))
+                copy(
+                    out=f_grouped[g][:].rearrange("p (r m j) -> p m j r", m=P, j=PACK)[:, part],
+                    in_=f0_raw[g][:].rearrange("p j (m r) -> p m j r", r=4)[:, part],
+                )
+            elif g == 4:
+                for n in range(first, last + 1):
+                    copy(
+                        out=f_grouped[4][:, 1024 * n : 1024 * (n + 1)].rearrange("p (r m j) -> p m j r", r=2, j=PACK),
+                        in_=f1_raw[:, n].rearrange("p j (m r) -> p m j r", r=2),
+                    )
+            else:
+                for s in range(first, last + 1):
+                    copy(
+                        out=f_grouped[5][:, 512 * s : 512 * (s + 1)].rearrange("p (w n j) -> p w n j", n=2, j=PACK),
+                        in_=f2_raw[:, :, s].rearrange("p n j w -> p w n j"),
+                    )
+
+        def quantize_features(g):
+            quantize(f_grouped[g], f_codes[g], f_scales[g], 0, CODE_COLUMNS[g])
+
+        def result_of_tile(g, t):
+            if g < 4:
+                return result[g][:].rearrange("p (a r j) -> p a r j", a=NA, r=4)[:, :, t, :]
+            if g == 4:
+                return result[4][:].rearrange("p (n a r j) -> p n a r j", n=2, a=NA, r=2)[:, t // 2, :, t % 2, :]
+            return result[5][:].rearrange("p (a j) -> p a j", a=NA)
+
+        def product(g, t, by_scalar=False):
+            if g < 4:
+                passes = [(P * t, w0_codes, w0_scales, 0)]
+                bias_tile = bias0[:]
+            elif g == 4:
+                passes = [(P * t, w12_codes, w12_scales, 0)]
+                bias_tile = bias12[:, 0, :]
+            else:
+                passes = [(0, w12_codes, w12_scales, O), (P, w12_codes, w12_scales, 2 * O)]
+                bias_tile = bias12[:, 1, :]
+            acc = ps_acc.tile([P, 512], F32, name="acc", tag="acc")
+            for n0, n1 in ((0, 256), (256, O)):
+                for i, (f_col, w_codes, w_scales, w_col) in enumerate(passes):
+                    nc.tensor.matmul_mx(
+                        out=acc[:, n0:n1],
+                        lhsT=f_codes[g][:, f_col : f_col + P].bitcast(FP8X4),
+                        lhsT_scale=f_scales[g][:, f_col : f_col + P],
+                        rhs=w_codes[:, w_col + n0 : w_col + n1].bitcast(FP8X4),
+                        rhs_scale=w_scales[:, w_col + n0 : w_col + n1],
+                        start=(i == 0),
+                        stop=(i == len(passes) - 1),
+                    )
+            sums = acc[:, 0:O].rearrange("p (a j) -> p a j", a=NA)
+            bias = bias_tile.rearrange("p (a j) -> p a j", a=NA)
+            if by_scalar:
+                nc.scalar.copy(out=result_of_tile(g, t), in_=sums)
+                nc.gpsimd.tensor_tensor(out=result_of_tile(g, t), in0=result_of_tile(g, t), in1=bias, op=ALU.add)
+            else:
+                nc.vector.tensor_tensor(out=result_of_tile(g, t), in0=sums, in1=bias, op=ALU.add)
+
+        anchors_of_rows = [anchors_0[:].rearrange("p a r c -> p (a r) c")] * 4 + [
+            anchors_1[:].rearrange("p n a r c -> p (n a r) c"),
+            anchors_x4[:, 12:18].rearrange("p (a c) -> p a c", c=2),
+        ]
+
+        def store_group(g, dst, tiles, as_bytes):
+            def view(ap):
+                return ap.bitcast(U8) if as_bytes else ap
+
+            if g < 4:
+                n, h = g // 2, g % 2
+                nc.sync.dma_start(
+                    out=dst[n, 0:ROWS_1, :].rearrange("(a h m r) j -> h m a (r j)", a=NA, h=2, r=4)[h],
+                    in_=view(tiles[g][:]).rearrange("p (a x) -> p a x", a=NA),
+                )
+            elif g == 4:
+                for n in range(2):
+                    store_level1(n, dst, tiles, as_bytes)
+            else:
+                for a in range(NA):
+                    nc.sync.dma_start(
+                        out=dst[:, ROWS_2 + 64 * a : ROWS_2 + 64 * (a + 1), :].rearrange("n w j -> w n j"),
+                        in_=view(tiles[5][:, P * a : P * (a + 1)]),
+                    )
+
+        def store_level1(n, dst, tiles, as_bytes):
+            ap = tiles[4][:, 2 * O * n : 2 * O * (n + 1)]
+            if as_bytes:
+                ap = ap.bitcast(U8)
+            nc.sync.dma_start(
+                out=dst[n, ROWS_1:ROWS_2, :].rearrange("(a m r) j -> m a (r j)", a=NA, r=2),
+                in_=ap.rearrange("p (a x) -> p a x", a=NA),
+            )
+
+        def finish(g):
+            rows = RESULT_COLUMNS[g] // P
+            by_row = result[g][:].rearrange("p (x j) -> p x j", j=P)
+            sig = keep.tile([P, rows, 4], F32, name="sig%d" % g)
+            nc.scalar.activation(out=sig[:], in_=by_row[:, :, 0:4], func=ACT.Sigmoid)
+            nc.gpsimd.tensor_scalar(
+                out=by_row[:, :, 0:2], in0=sig[:, :, 0:2], scalar1=2.0, scalar2=-0.5, op0=ALU.mult, op1=ALU.add
+            )
+            scaled = keep.tile([P, rows, 2], F32, name="scaled%d" % g)
+            nc.gpsimd.tensor_tensor(out=scaled[:], in0=sig[:, :, 2:4], in1=anchors_of_rows[g], op=ALU.mult)
+            nc.gpsimd.tensor_tensor(out=by_row[:, :, 2:4], in0=scaled[:], in1=sig[:, :, 2:4], op=ALU.mult)
+            store_group(g, out_0, result, False)
+
+        def reduce_abs(g):
+            nc.vector.tensor_reduce(
+                out=maxima[:, g : g + 1], in_=result[g][:], axis=AX.X, op=ALU.max, apply_absolute_value=True
+            )
+
+        by_vector = nc.vector.tensor_copy
+        on_scalar = nc.scalar.copy
+
+        turn_weights(w0_units[0:2], w0_grouped, 0)
+        turn_weights(w0_units[2:3], w0_grouped, 2)
+        spread_bias0()
+        interleave(0, by_vector, 0, 1)
+        spread_anchors()
+        interleave(2, on_scalar, 0, 0)
+        quantize_features(0)
+        interleave(1, by_vector, 0, 1)
+        quantize(w0_grouped, w0_codes, w0_scales, 0, 256)
+        quantize(w0_grouped, w0_codes, w0_scales, 256, O)
+        quantize_features(1)
+
+        for t in range(4):
+            product(0, t)
+        interleave(2, on_scalar, 1, 1)
+        product(1, 0)
+        product(1, 1)
+        quantize_features(2)
+        interleave(3, on_scalar, 0, 0)
+        finish(0)
+        product(1, 2)
+        product(1, 3)
+        interleave(3, on_scalar, 1, 1)
+        turn_w12(0)
+        product(2, 0)
+        product(2, 1)
+        interleave(5, on_scalar, 0, 0)
+        quantize_features(3)
+        product(2, 2)
+        product(2, 3)
+        finish(1)
+        interleave(5, on_scalar, 1, 1)
+        reduce_abs(0)
+        turn_w12(1)
+        product(3, 0)
+        product(3, 1, by_scalar=True)
+        finish(2)
+        interleave(4, on_scalar, 0, 0)
+        turn_w12(2)
+        reduce_abs(1)
+        product(3, 2)
+        product(3, 3)
+        quantize_features(5)
+        turn_w12(3)
+        turn_w12(4)
+        interleave(4, on_scalar, 1, 1)
+        quantize(w12_grouped, w12_codes, w12_scales, 0, 1024)
+        quantize(w12_grouped, w12_codes, w12_scales, 1024, 3 * O)
+        quantize_features(4)
+        reduce_abs(2)
+        finish(3)
+        product(4, 0, by_scalar=True)
+        product(4, 1)
+        product(4, 2)
+        product(4, 3)
+        reduce_abs(3)
+        product(5, 0)
+        finish(4)
+        finish(5)
+        reduce_abs(4)
+        reduce_abs(5)
+
+        partition_max = keep.tile([P, 1], F32, name="partition_max")
+        nc.vector.tensor_reduce(out=partition_max[:], in_=maxima[:, 0:6], axis=AX.X, op=ALU.max)
+        all_maxima = ps_turn.tile([P, P], F32, name="all_maxima", tag="turn")
+        nc.tensor.transpose(all_maxima[:], partition_max[:, 0:1].to_broadcast([P, P]), ident[:])
+        amax = keep.tile([P, 1], F32, name="amax")
+        nc.vector.tensor_reduce(out=amax[:], in_=all_maxima[:], axis=AX.X, op=ALU.max)
+        inverse = keep.tile([P, 1], F32, name="inverse")
+        nc.vector.reciprocal(out=inverse[:], in_=amax[:])
+        factor = keep.tile([P, 1], F32, name="factor")
+        nc.vector.tensor_scalar(out=factor[:], in0=inverse[:], scalar1=FP8_MAX, scalar2=None, op0=ALU.mult)
+
+        def cast_on_vector(g, c0, c1):
+            nc.vector.tensor_scalar(
+                out=result_fp8[g][:, c0:c1],
+                in0=result[g][:, c0:c1],
+                scalar1=factor[:, 0:1],
+                scalar2=None,
+                op0=ALU.mult,
+                saturate=False,
+            )
+
+        def cast_on_scalar(g, c0, c1):
+            nc.scalar.activation(
+                out=result_fp8[g][:, c0:c1],
+                in_=result[g][:, c0:c1],
+                func=ACT.Identity,
+                scale=factor[:, 0:1],
+                bias=zero[:, 0:1],
+                saturate=False,
+            )
+
+        cast_on_scalar(5, 0, O)
+        cast_on_vector(0, 0, 4 * O)
+        store_group(5, out_1, result_fp8, True)
+        store_group(0, out_1, result_fp8, True)
+        cast_on_scalar(3, 0, 4 * O)
+        cast_on_vector(1, 0, 4 * O)
+        store_group(1, out_1, result_fp8, True)
+        store_group(3, out_1, result_fp8, True)
+        cast_on_vector(2, 0, 4 * O)
+        store_group(2, out_1, result_fp8, True)
+        cast_on_scalar(4, 2 * O, 4 * O)
+        store_level1(1, out_1, result_fp8, True)
+        cast_on_vector(4, 0, 2 * O)
+        store_level1(0, out_1, result_fp8, True)

@@ -31,8 +31,8 @@ def tile_head_kernel(tc, f0, f1, f2, w0, b0, w1, b1, w2, b2, anchors, out_0, out
     nc = tc.nc
     with ExitStack() as ctx:
         keep = ctx.enter_context(tc.tile_pool(name="keep", bufs=1))
-        ps_turn = ctx.enter_context(tc.psum_pool(name="ps_turn", bufs=5))
-        ps_acc = ctx.enter_context(tc.psum_pool(name="ps_acc", bufs=3))
+        ps_turn = ctx.enter_context(tc.psum_pool(name="ps_turn", bufs=4))
+        ps_acc = ctx.enter_context(tc.psum_pool(name="ps_acc", bufs=4))
         ctx.enter_context(tc.manual_schedule())
 
         b0_row = keep.tile([1, O], BF16, name="b0_row")

@@ -38,7 +38,6 @@ def tile_head_kernel(tc, f0, f1, f2, w0, b0, w1, b1, w2, b2, anchors, out_0, out
         b0_row = keep.tile([1, O], BF16, name="b0_row")
         nc.sync.dma_start(out=b0_row[0:1, :], in_=b0.rearrange("(x o) -> x o", x=1))
         anchors_bf = keep.tile([P, 18], BF16, name="anchors_bf")
-        nc.scalar.dma_start(out=anchors_bf[:], in_=anchors.rearrange("l a c -> (l a c)").partition_broadcast(P))
         w0_raw = keep.tile([P, NA, 512], BF16, name="w0_raw")
         f0_raw = []
         for n in range(2):
@@ -49,6 +48,7 @@ def tile_head_kernel(tc, f0, f1, f2, w0, b0, w1, b1, w2, b2, anchors, out_0, out
                 f0_raw.append(half)
                 if n == 0 and h == 0:
                     nc.sync.dma_start(out=w0_raw[:], in_=w0.rearrange("(a p) k -> p a k", p=P))
+        nc.sync.dma_start(out=anchors_bf[:], in_=anchors.rearrange("l a c -> (l a c)").partition_broadcast(P))
         w1_raw = keep.tile([P, NA, 512], BF16, name="w1_raw")
         nc.sync.dma_start(out=w1_raw[:], in_=w1.rearrange("(a p) k -> p a k", p=P))
         w2_raw = keep.tile([P, NA, 1024], BF16, name="w2_raw")
@@ -133,13 +133,12 @@ def tile_head_kernel(tc, f0, f1, f2, w0, b0, w1, b1, w2, b2, anchors, out_0, out
         def turn_w12(pair):
             turn_weights(w12_units[2 * pair : 2 * pair + 2], w12_grouped, 2 * pair)
 
-        maxima = keep.tile([P, 8], F32, name="maxima")
         f_grouped = [
             keep.tile([P, PACK * c], BF16, name="f_grouped%d" % g, align_bytes=64) for g, c in enumerate(CODE_COLUMNS)
         ]
         f_codes = [keep.tile([P, c], U32, name="f_codes%d" % g, align_bytes=64) for g, c in enumerate(CODE_COLUMNS)]
         f_scales = [keep.tile([P, c], U8, name="f_scales%d" % g, align_bytes=64) for g, c in enumerate(CODE_COLUMNS)]
-        result = [keep.tile([P, c], F32, name="result%d" % g) for g, c in enumerate(RESULT_COLUMNS)]
+        result = [keep.tile([P, c + (8 if g == 5 else 0)], F32, name="result%d" % g) for g, c in enumerate(RESULT_COLUMNS)]
         result_fp8 = [keep.tile([P, c], FP8, name="result_fp8_%d" % g) for g, c in enumerate(RESULT_COLUMNS)]
 
         def interleave(g, copy, first, last):
@@ -170,7 +169,7 @@ def tile_head_kernel(tc, f0, f1, f2, w0, b0, w1, b1, w2, b2, anchors, out_0, out
                 return result[g][:].rearrange("p (a r j) -> p a r j", a=NA, r=4)[:, :, t, :]
             if g == 4:
                 return result[4][:].rearrange("p (n a r j) -> p n a r j", n=2, a=NA, r=2)[:, t // 2, :, t % 2, :]
-            return result[5][:].rearrange("p (a j) -> p a j", a=NA)
+            return result[5][:, 0:O].rearrange("p (a j) -> p a j", a=NA)
 
         def product(g, t, by_scalar=False):
             if g < 4:
@@ -238,7 +237,7 @@ def tile_head_kernel(tc, f0, f1, f2, w0, b0, w1, b1, w2, b2, anchors, out_0, out
 
         def finish(g):
             rows = RESULT_COLUMNS[g] // P
-            by_row = result[g][:].rearrange("p (x j) -> p x j", j=P)
+            by_row = result[g][:, 0 : RESULT_COLUMNS[g]].rearrange("p (x j) -> p x j", j=P)
             sig = keep.tile([P, rows, 4], F32, name="sig%d" % g)
             nc.scalar.activation(out=sig[:], in_=by_row[:, :, 0:4], func=ACT.Sigmoid)
             nc.gpsimd.tensor_scalar(
@@ -249,10 +248,17 @@ def tile_head_kernel(tc, f0, f1, f2, w0, b0, w1, b1, w2, b2, anchors, out_0, out
             nc.gpsimd.tensor_tensor(out=by_row[:, :, 2:4], in0=scaled[:], in1=sig[:, :, 2:4], op=ALU.mult)
             store_group(g, out_0, result, False)
 
+        partition_max = keep.tile([P, 1], F32, name="partition_max")
+
         def reduce_abs(g):
-            nc.vector.tensor_reduce(
-                out=maxima[:, g : g + 1], in_=result[g][:], axis=AX.X, op=ALU.max, apply_absolute_value=True
-            )
+            if g < 5:
+                nc.vector.tensor_reduce(
+                    out=result[5][:, O + g : O + g + 1], in_=result[g][:], axis=AX.X, op=ALU.max, apply_absolute_value=True
+                )
+            else:
+                nc.vector.tensor_reduce(
+                    out=partition_max[:], in_=result[5][:, 0 : O + 5], axis=AX.X, op=ALU.max, apply_absolute_value=True
+                )
 
         by_vector = nc.vector.tensor_copy
         on_scalar = nc.scalar.copy
@@ -261,8 +267,8 @@ def tile_head_kernel(tc, f0, f1, f2, w0, b0, w1, b1, w2, b2, anchors, out_0, out
         turn_weights(w0_units[2:3], w0_grouped, 2)
         spread_bias0()
         interleave(0, by_vector, 0, 1)
-        spread_anchors()
         interleave(2, on_scalar, 0, 0)
+        spread_anchors()
         quantize_features(0)
         interleave(1, by_vector, 0, 1)
         quantize(w0_grouped, w0_codes, w0_scales, 0, 256)
@@ -319,16 +325,21 @@ def tile_head_kernel(tc, f0, f1, f2, w0, b0, w1, b1, w2, b2, anchors, out_0, out
         reduce_abs(4)
         reduce_abs(5)
 
-        partition_max = keep.tile([P, 1], F32, name="partition_max")
-        nc.vector.tensor_reduce(out=partition_max[:], in_=maxima[:, 0:6], axis=AX.X, op=ALU.max)
         all_maxima = ps_turn.tile([P, P], F32, name="all_maxima", tag="turn")
         nc.tensor.transpose(all_maxima[:], partition_max[:, 0:1].to_broadcast([P, P]), ident[:])
-        amax = keep.tile([P, 1], F32, name="amax")
-        nc.vector.tensor_reduce(out=amax[:], in_=all_maxima[:], axis=AX.X, op=ALU.max)
-        inverse = keep.tile([P, 1], F32, name="inverse")
-        nc.vector.reciprocal(out=inverse[:], in_=amax[:])
+        scaled_maxima = keep.tile([P, P], F32, name="scaled_maxima")
+        scale = keep.tile([P, 1], F32, name="scale")
+        nc.vector.tensor_scalar(
+            out=scaled_maxima[:],
+            in0=all_maxima[:],
+            scalar1=1.0 / FP8_MAX,
+            scalar2=None,
+            op0=ALU.mult,
+            op1=ALU.max,
+            accum_out=scale[:],
+        )
         factor = keep.tile([P, 1], F32, name="factor")
-        nc.vector.tensor_scalar(out=factor[:], in0=inverse[:], scalar1=FP8_MAX, scalar2=None, op0=ALU.mult)
+        nc.vector.reciprocal(out=factor[:], in_=scale[:])
 
         def cast_on_vector(g, c0, c1):
             nc.vector.tensor_scalar(

@@ -36,7 +36,6 @@ def tile_head_kernel(tc, f0, f1, f2, w0, b0, w1, b1, w2, b2, anchors, out_0, out
         ctx.enter_context(tc.manual_schedule())
 
         b0_row = keep.tile([1, O], BF16, name="b0_row")
-        nc.sync.dma_start(out=b0_row[0:1, :], in_=b0.rearrange("(x o) -> x o", x=1))
         anchors_bf = keep.tile([P, 18], BF16, name="anchors_bf")
         w0_raw = keep.tile([P, NA, 512], BF16, name="w0_raw")
         f0_raw = []
@@ -48,6 +47,7 @@ def tile_head_kernel(tc, f0, f1, f2, w0, b0, w1, b1, w2, b2, anchors, out_0, out
                 f0_raw.append(half)
                 if n == 0 and h == 0:
                     nc.sync.dma_start(out=w0_raw[:], in_=w0.rearrange("(a p) k -> p a k", p=P))
+                    nc.sync.dma_start(out=b0_row[0:1, :], in_=b0.rearrange("(x o) -> x o", x=1))
         nc.sync.dma_start(out=anchors_bf[:], in_=anchors.rearrange("l a c -> (l a c)").partition_broadcast(P))
         w1_raw = keep.tile([P, NA, 512], BF16, name="w1_raw")
         nc.sync.dma_start(out=w1_raw[:], in_=w1.rearrange("(a p) k -> p a k", p=P))
@@ -78,7 +78,7 @@ def tile_head_kernel(tc, f0, f1, f2, w0, b0, w1, b1, w2, b2, anchors, out_0, out
         nc.vector.memset(ones[:], 1.0)
         ident = keep.tile([P, P], F32, name="ident")
         make_identity(nc, ident[:])
-        nc.vector.tensor_copy(out=b0_rows[0:1, :], in_=b0_row[0:1, :])
+        nc.scalar.copy(out=b0_rows[0:1, :], in_=b0_row[0:1, :])
 
         bias0 = keep.tile([P, O], F32, name="bias0")
         anchors_x4 = keep.tile([P, 18], F32, name="anchors_x4")

from contextlib import ExitStack

import concourse.mybir as mybir
from concourse.masks import make_identity

F32 = mybir.dt.float32
BF16 = mybir.dt.bfloat16
U32 = mybir.dt.uint32
U8 = mybir.dt.uint8
FP8X4 = mybir.dt.float8_e4m3fn_x4
FP8 = mybir.dt.float8_e4m3fn
ALU = mybir.AluOpType
ACT = mybir.ActivationFunctionType
AX = mybir.AxisListType

P = 128
PACK = 4
NA = 3
O = NA * P
ROWS_1 = 3072
ROWS_2 = 3840
FP8_MAX = 448.0

FLOPS = 2 * O * (512 * 2048 + 512 * 512 + 1024 * 128)

CODE_COLUMNS = [512, 512, 512, 512, 512, 256]
RESULT_COLUMNS = [4 * O, 4 * O, 4 * O, 4 * O, 4 * O, O]


def tile_head_kernel(tc, f0, f1, f2, w0, b0, w1, b1, w2, b2, anchors, out_0, out_1):
    nc = tc.nc
    with ExitStack() as ctx:
        keep = ctx.enter_context(tc.tile_pool(name="keep", bufs=1))
        ps_turn = ctx.enter_context(tc.psum_pool(name="ps_turn", bufs=4))
        ps_acc = ctx.enter_context(tc.psum_pool(name="ps_acc", bufs=4))
        ctx.enter_context(tc.manual_schedule())

        b0_row = keep.tile([1, O], BF16, name="b0_row")
        anchors_bf = keep.tile([P, 18], BF16, name="anchors_bf")
        w0_raw = keep.tile([P, NA, 512], BF16, name="w0_raw")
        f0_raw = []
        for n in range(2):
            image = f0[n].rearrange("(p j) u v -> p j (u v)", j=PACK)
            for h in range(2):
                half = keep.tile([P, PACK, 512], BF16, name="f0_raw%d%d" % (n, h))
                nc.sync.dma_start(out=half[:], in_=image[:, :, 512 * h : 512 * (h + 1)])
                f0_raw.append(half)
                if n == 0 and h == 0:
                    nc.sync.dma_start(out=w0_raw[:], in_=w0.rearrange("(a p) k -> p a k", p=P))
                    nc.sync.dma_start(out=b0_row[0:1, :], in_=b0.rearrange("(x o) -> x o", x=1))
        nc.sync.dma_start(out=anchors_bf[:], in_=anchors.rearrange("l a c -> (l a c)").partition_broadcast(P))
        w1_raw = keep.tile([P, NA, 512], BF16, name="w1_raw")
        nc.sync.dma_start(out=w1_raw[:], in_=w1.rearrange("(a p) k -> p a k", p=P))
        w2_raw = keep.tile([P, NA, 1024], BF16, name="w2_raw")
        nc.sync.dma_start(out=w2_raw[:], in_=w2.rearrange("(a p) k -> p a k", p=P))
        f1_raw = keep.tile([P, 2, PACK, 256], BF16, name="f1_raw")
        nc.sync.dma_start(
            out=f1_raw[:].rearrange("p n j w -> p n (j w)"),
            in_=f1.rearrange("n (p j) u v -> p n (j u v)", j=PACK),
        )
        f2_raw = keep.tile([P, 2, 2, PACK, 64], BF16, name="f2_raw")
        for n in range(2):
            nc.sync.dma_start(
                out=f2_raw[:, n].rearrange("p s j w -> p s (j w)"),
                in_=f2[n].rearrange("(s p j) u v -> p s (j u v)", s=2, j=PACK),
            )
        bias12 = keep.tile([P, 2, O], BF16, name="bias12")
        nc.sync.dma_start(out=bias12[:, 0, :], in_=b1.partition_broadcast(P))
        nc.sync.dma_start(out=bias12[:, 1, :], in_=b2.partition_broadcast(P))

        zero = keep.tile([P, 1], F32, name="zero")
        nc.vector.memset(zero[:], 0.0)
        warm = keep.tile([P, 1], F32, name="warm")
        nc.scalar.activation(out=warm[:], in_=zero[:], func=ACT.Sigmoid)
        b0_rows = keep.tile([P, O], BF16, name="b0_rows")
        nc.vector.memset(b0_rows[:], 0.0)
        ones = keep.tile([P, P], BF16, name="ones")
        nc.vector.memset(ones[:], 1.0)
        ident = keep.tile([P, P], F32, name="ident")
        make_identity(nc, ident[:])
        nc.scalar.copy(out=b0_rows[0:1, :], in_=b0_row[0:1, :])

        bias0 = keep.tile([P, O], F32, name="bias0")
        anchors_x4 = keep.tile([P, 18], F32, name="anchors_x4")
        anchors_0 = keep.tile([P, NA, 4, 2], F32, name="anchors_0")
        anchors_1 = keep.tile([P, 2, NA, 2, 2], F32, name="anchors_1")

        def spread_bias0():
            bank = ps_turn.tile([P, 512], F32, name="bank", tag="turn")
            nc.tensor.matmul(bank[:, 0:O], lhsT=ones[:], rhs=b0_rows[:], start=True, stop=True)
            nc.scalar.copy(out=bias0[:], in_=bank[:, 0:O])

        def spread_anchors():
            nc.scalar.activation(out=anchors_x4[:], in_=anchors_bf[:], func=ACT.Copy, scale=4.0)
            for r in range(4):
                nc.gpsimd.tensor_copy(
                    out=anchors_0[:, :, r, :], in_=anchors_x4[:, 0:6].rearrange("p (a c) -> p a c", c=2)
                )
            for n in range(2):
                for r in range(2):
                    nc.gpsimd.tensor_copy(
                        out=anchors_1[:, n, :, r, :], in_=anchors_x4[:, 6:12].rearrange("p (a c) -> p a c", c=2)
                    )

        def turn_weights(units, grouped, first):
            words_out = grouped[:].bitcast(F32).rearrange("p (q r u) -> p q r u", r=P, u=2)
            turned = ps_turn.tile([P, 2, 2, P], F32, name="turned", tag="turn")
            for i, (raw, a, s) in enumerate(units):
                words = raw[:, a, :].bitcast(F32)
                for u in range(2):
                    nc.tensor.transpose(turned[:, i, u, :], words[:, 256 * s + u : 256 * (s + 1) : 2], ident[:])
            nc.scalar.copy(
                out=words_out[:, first : first + len(units), :, :],
                in_=turned[:, 0 : len(units)].rearrange("p i u r -> p i r u"),
            )

        def quantize(grouped, codes, scales, c0, c1):
            nc.vector.quantize_mx(
                out=codes[:, c0:c1].bitcast(FP8X4),
                scales=scales[:, c0:c1],
                in_=grouped[:, PACK * c0 : PACK * c1],
            )

        w0_grouped = keep.tile([P, PACK * O], BF16, name="w0_grouped", align_bytes=64)
        w0_codes = keep.tile([P, O], U32, name="w0_codes", align_bytes=64)
        w0_scales = keep.tile([P, O], U8, name="w0_scales", align_bytes=64)
        w12_grouped = keep.tile([P, PACK * 3 * O], BF16, name="w12_grouped", align_bytes=64)
        w12_codes = keep.tile([P, 3 * O], U32, name="w12_codes", align_bytes=64)
        w12_scales = keep.tile([P, 3 * O], U8, name="w12_scales", align_bytes=64)
        w0_units = [(w0_raw, a, 0) for a in range(NA)]
        w12_units = [(w1_raw, a, 0) for a in range(NA)] + [(w2_raw, a, s) for s in range(2) for a in range(NA)]

        def turn_w12(pair):
            turn_weights(w12_units[2 * pair : 2 * pair + 2], w12_grouped, 2 * pair)

        f_grouped = [
            keep.tile([P, PACK * c], BF16, name="f_grouped%d" % g, align_bytes=64) for g, c in enumerate(CODE_COLUMNS)
        ]
        f_codes = [keep.tile([P, c], U32, name="f_codes%d" % g, align_bytes=64) for g, c in enumerate(CODE_COLUMNS)]
        f_scales = [keep.tile([P, c], U8, name="f_scales%d" % g, align_bytes=64) for g, c in enumerate(CODE_COLUMNS)]
        result = [keep.tile([P, c + (8 if g == 5 else 0)], F32, name="result%d" % g) for g, c in enumerate(RESULT_COLUMNS)]
        result_fp8 = [keep.tile([P, c], FP8, name="result_fp8_%d" % g) for g, c in enumerate(RESULT_COLUMNS)]

        def interleave(g, copy, first, last):
            if g < 4:
                part = slice(64 * first, 64 * (last + 1))
                copy(
                    out=f_grouped[g][:].rearrange("p (r m j) -> p m j r", m=P, j=PACK)[:, part],
                    in_=f0_raw[g][:].rearrange("p j (m r) -> p m j r", r=4)[:, part],
                )
            elif g == 4:
                for n in range(first, last + 1):
                    copy(
                        out=f_grouped[4][:, 1024 * n : 1024 * (n + 1)].rearrange("p (r m j) -> p m j r", r=2, j=PACK),
                        in_=f1_raw[:, n].rearrange("p j (m r) -> p m j r", r=2),
                    )
            else:
                for s in range(first, last + 1):
                    copy(
                        out=f_grouped[5][:, 512 * s : 512 * (s + 1)].rearrange("p (w n j) -> p w n j", n=2, j=PACK),
                        in_=f2_raw[:, :, s].rearrange("p n j w -> p w n j"),
                    )

        def quantize_features(g):
            quantize(f_grouped[g], f_codes[g], f_scales[g], 0, CODE_COLUMNS[g])

        def result_of_tile(g, t):
            if g < 4:
                return result[g][:].rearrange("p (a r j) -> p a r j", a=NA, r=4)[:, :, t, :]
            if g == 4:
                return result[4][:].rearrange("p (n a r j) -> p n a r j", n=2, a=NA, r=2)[:, t // 2, :, t % 2, :]
            return result[5][:, 0:O].rearrange("p (a j) -> p a j", a=NA)

        def product(g, t, by_scalar=False):
            if g < 4:
                passes = [(P * t, w0_codes, w0_scales, 0)]
                bias_tile = bias0[:]
            elif g == 4:
                passes = [(P * t, w12_codes, w12_scales, 0)]
                bias_tile = bias12[:, 0, :]
            else:
                passes = [(0, w12_codes, w12_scales, O), (P, w12_codes, w12_scales, 2 * O)]
                bias_tile = bias12[:, 1, :]
            acc = ps_acc.tile([P, 512], F32, name="acc", tag="acc")
            for n0, n1 in ((0, 256), (256, O)):
                for i, (f_col, w_codes, w_scales, w_col) in enumerate(passes):
                    nc.tensor.matmul_mx(
                        out=acc[:, n0:n1],
                        lhsT=f_codes[g][:, f_col : f_col + P].bitcast(FP8X4),
                        lhsT_scale=f_scales[g][:, f_col : f_col + P],
                        rhs=w_codes[:, w_col + n0 : w_col + n1].bitcast(FP8X4),
                        rhs_scale=w_scales[:, w_col + n0 : w_col + n1],
                        start=(i == 0),
                        stop=(i == len(passes) - 1),
                    )
            sums = acc[:, 0:O].rearrange("p (a j) -> p a j", a=NA)
            bias = bias_tile.rearrange("p (a j) -> p a j", a=NA)
            if by_scalar:
                nc.scalar.copy(out=result_of_tile(g, t), in_=sums)
                nc.gpsimd.tensor_tensor(out=result_of_tile(g, t), in0=result_of_tile(g, t), in1=bias, op=ALU.add)
            else:
                nc.vector.tensor_tensor(out=result_of_tile(g, t), in0=sums, in1=bias, op=ALU.add)

        anchors_of_rows = [anchors_0[:].rearrange("p a r c -> p (a r) c")] * 4 + [
            anchors_1[:].rearrange("p n a r c -> p (n a r) c"),
            anchors_x4[:, 12:18].rearrange("p (a c) -> p a c", c=2),
        ]

        def store_group(g, dst, tiles, as_bytes):
            def view(ap):
                return ap.bitcast(U8) if as_bytes else ap

            if g < 4:
                n, h = g // 2, g % 2
                nc.sync.dma_start(
                    out=dst[n, 0:ROWS_1, :].rearrange("(a h m r) j -> h m a (r j)", a=NA, h=2, r=4)[h],
                    in_=view(tiles[g][:]).rearrange("p (a x) -> p a x", a=NA),
                )
            elif g == 4:
                for n in range(2):
                    store_level1(n, dst, tiles, as_bytes)
            else:
                for a in range(NA):
                    nc.sync.dma_start(
                        out=dst[:, ROWS_2 + 64 * a : ROWS_2 + 64 * (a + 1), :].rearrange("n w j -> w n j"),
                        in_=view(tiles[5][:, P * a : P * (a + 1)]),
                    )

        def store_level1(n, dst, tiles, as_bytes):
            ap = tiles[4][:, 2 * O * n : 2 * O * (n + 1)]
            if as_bytes:
                ap = ap.bitcast(U8)
            nc.sync.dma_start(
                out=dst[n, ROWS_1:ROWS_2, :].rearrange("(a m r) j -> m a (r j)", a=NA, r=2),
                in_=ap.rearrange("p (a x) -> p a x", a=NA),
            )

        def finish(g):
            rows = RESULT_COLUMNS[g] // P
            by_row = result[g][:, 0 : RESULT_COLUMNS[g]].rearrange("p (x j) -> p x j", j=P)
            sig = keep.tile([P, rows, 4], F32, name="sig%d" % g)
            nc.scalar.activation(out=sig[:], in_=by_row[:, :, 0:4], func=ACT.Sigmoid)
            nc.gpsimd.tensor_scalar(
                out=by_row[:, :, 0:2], in0=sig[:, :, 0:2], scalar1=2.0, scalar2=-0.5, op0=ALU.mult, op1=ALU.add
            )
            scaled = keep.tile([P, rows, 2], F32, name="scaled%d" % g)
            nc.gpsimd.tensor_tensor(out=scaled[:], in0=sig[:, :, 2:4], in1=anchors_of_rows[g], op=ALU.mult)
            nc.gpsimd.tensor_tensor(out=by_row[:, :, 2:4], in0=scaled[:], in1=sig[:, :, 2:4], op=ALU.mult)
            store_group(g, out_0, result, False)

        partition_max = keep.tile([P, 1], F32, name="partition_max")

        def reduce_abs(g):
            if g < 5:
                nc.vector.tensor_reduce(
                    out=result[5][:, O + g : O + g + 1], in_=result[g][:], axis=AX.X, op=ALU.max, apply_absolute_value=True
                )
            else:
                nc.vector.tensor_reduce(
                    out=partition_max[:], in_=result[5][:, 0 : O + 5], axis=AX.X, op=ALU.max, apply_absolute_value=True
                )

        by_vector = nc.vector.tensor_copy
        on_scalar = nc.scalar.copy

        turn_weights(w0_units[0:2], w0_grouped, 0)
        turn_weights(w0_units[2:3], w0_grouped, 2)
        spread_bias0()
        interleave(0, by_vector, 0, 1)
        interleave(2, on_scalar, 0, 0)
        spread_anchors()
        quantize_features(0)
        interleave(1, by_vector, 0, 1)
        quantize(w0_grouped, w0_codes, w0_scales, 0, 256)
        quantize(w0_grouped, w0_codes, w0_scales, 256, O)
        quantize_features(1)

        for t in range(4):
            product(0, t)
        interleave(2, on_scalar, 1, 1)
        product(1, 0)
        product(1, 1)
        quantize_features(2)
        interleave(3, on_scalar, 0, 0)
        finish(0)
        product(1, 2)
        product(1, 3)
        interleave(3, on_scalar, 1, 1)
        turn_w12(0)
        product(2, 0)
        product(2, 1)
        interleave(5, on_scalar, 0, 0)
        quantize_features(3)
        product(2, 2)
        product(2, 3)
        finish(1)
        interleave(5, on_scalar, 1, 1)
        reduce_abs(0)
        turn_w12(1)
        product(3, 0)
        product(3, 1, by_scalar=True)
        finish(2)
        interleave(4, on_scalar, 0, 0)
        turn_w12(2)
        reduce_abs(1)
        product(3, 2)
        product(3, 3)
        quantize_features(5)
        turn_w12(3)
        turn_w12(4)
        interleave(4, on_scalar, 1, 1)
        quantize(w12_grouped, w12_codes, w12_scales, 0, 1024)
        quantize(w12_grouped, w12_codes, w12_scales, 1024, 3 * O)
        quantize_features(4)
        reduce_abs(2)
        finish(3)
        product(4, 0, by_scalar=True)
        product(4, 1)
        product(4, 2)
        product(4, 3)
        reduce_abs(3)
        product(5, 0)
        finish(4)
        finish(5)
        reduce_abs(4)
        reduce_abs(5)

        all_maxima = ps_turn.tile([P, P], F32, name="all_maxima", tag="turn")
        nc.tensor.transpose(all_maxima[:], partition_max[:, 0:1].to_broadcast([P, P]), ident[:])
        scaled_maxima = keep.tile([P, P], F32, name="scaled_maxima")
        scale = keep.tile([P, 1], F32, name="scale")
        nc.vector.tensor_scalar(
            out=scaled_maxima[:],
            in0=all_maxima[:],
            scalar1=1.0 / FP8_MAX,
            scalar2=None,
            op0=ALU.mult,
            op1=ALU.max,
            accum_out=scale[:],
        )
        factor = keep.tile([P, 1], F32, name="factor")
        nc.vector.reciprocal(out=factor[:], in_=scale[:])

        def cast_on_vector(g, c0, c1):
            nc.vector.tensor_scalar(
                out=result_fp8[g][:, c0:c1],
                in0=result[g][:, c0:c1],
                scalar1=factor[:, 0:1],
                scalar2=None,
                op0=ALU.mult,
                saturate=False,
            )

        def cast_on_scalar(g, c0, c1):
            nc.scalar.activation(
                out=result_fp8[g][:, c0:c1],
                in_=result[g][:, c0:c1],
                func=ACT.Identity,
                scale=factor[:, 0:1],
                bias=zero[:, 0:1],
                saturate=False,
            )

        cast_on_scalar(5, 0, O)
        cast_on_vector(0, 0, 4 * O)
        store_group(5, out_1, result_fp8, True)
        store_group(0, out_1, result_fp8, True)
        cast_on_scalar(3, 0, 4 * O)
        cast_on_vector(1, 0, 4 * O)
        store_group(1, out_1, result_fp8, True)
        store_group(3, out_1, result_fp8, True)
        cast_on_vector(2, 0, 4 * O)
        store_group(2, out_1, result_fp8, True)
        cast_on_scalar(4, 2 * O, 4 * O)
        store_level1(1, out_1, result_fp8, True)
        cast_on_vector(4, 0, 2 * O)
        store_level1(0, out_1, result_fp8, True)
